import numpy as np
import ml_dtypes


def mxq(x, axis, fmt="e4m3"):
    dtype, down = {"e4m3": (ml_dtypes.float8_e4m3fn, 7), "e5m2": (ml_dtypes.float8_e5m2, 14)}[fmt]
    v = np.moveaxis(np.asarray(x, np.float32).astype(ml_dtypes.bfloat16).astype(np.float64), axis, -1)
    blocks = v.reshape(v.shape[:-1] + (-1, 32))
    amax = np.abs(blocks).max(-1, keepdims=True)
    byte = np.maximum(np.where(amax > 0, np.frexp(amax)[1] - 1 + 127, 0) - down, 1)
    scale = np.exp2(byte - 127.0)
    codes = (blocks / scale).astype(np.float32).astype(dtype).astype(np.float64)
    return np.moveaxis((codes * scale).reshape(v.shape), -1, axis)


WIDE = False


def mx_kscale(k):
    if not WIDE:
        return np.ones(k)
    levels = np.array([10, -10, 5, -5, 0])
    a = np.random.permutation(np.resize(levels, k // 512 * 4)).reshape(k // 512, 4)
    idx = np.arange(k)
    return np.exp2(a[idx // 512, idx % 128 // 32])


BF16 = ml_dtypes.bfloat16


def bf(x):
    return np.asarray(x, np.float32).astype(BF16)


def f64(x):
    return np.asarray(x).astype(np.float64)


M, N0, N1, N2, N3, R0, R1, R2, R3, R4 = 8192, 128, 8, 1, 128, 1, 128, 512, 128, 1
IN = N0 * N1
OUT = N2 * N3 * R4


def setup_inputs():
    s = mx_kscale(IN)
    return {"x": bf(np.random.standard_normal((M, IN)) * s),
            "tt_prefix": bf(np.random.standard_normal((IN * N2, R3)) / np.repeat(s, N2)[:, None]),
            "core3": bf(np.random.standard_normal((R3, N3, R4)) / np.sqrt(R3 * IN))}


def reference(x, tt_prefix, core3):
    w = (f64(tt_prefix) @ f64(core3).reshape(R3, N3 * R4)).reshape(IN, OUT)
    return mxq(f64(x), 1, "e4m3") @ mxq(w, 0, "e4m3")

@@ -1,0 +1,179 @@
+import concourse.mybir as mybir
+from concourse.masks import make_identity
+
+F32 = mybir.dt.float32
+BF16 = mybir.dt.bfloat16
+U32 = mybir.dt.uint32
+U8 = mybir.dt.uint8
+FP8X4 = mybir.dt.float8_e4m3fn_x4
+
+P = 128
+ROWS = 8192
+K = 1024
+N = 128
+RANK = 128
+TILES = ROWS // P
+WORDS = K // 2
+QUAD = 4
+STEPS = TILES // QUAD
+XT_BANKS = 6
+LOADS = [2, 2] + [4] * 14 + [2, 2]
+STORES = [4, 4, 4, 2, 1, 1]
+
+FLOPS = 2 * ROWS * K * N + 2 * K * RANK * N
+
+
+def tile_tttlayer_pb_t_kernel(tc, x, tt_prefix, core3, out):
+    nc = tc.nc
+    x_view = x.rearrange("(p t) k -> p t k", t=TILES)
+    out_view = out.rearrange("(p t) n -> p t n", t=TILES)
+
+    with tc.tile_pool(name="const", bufs=1) as const, tc.tile_pool(
+        name="xin", bufs=1
+    ) as xin, tc.tile_pool(name="work", bufs=1) as work, tc.tile_pool(
+        name="res", bufs=1
+    ) as res, tc.psum_pool(name="psum", bufs=1) as psum, tc.manual_schedule():
+        core_sb = const.tile([P, N], BF16, name="core_sb")
+        nc.scalar.dma_start(out=core_sb[:], in_=core3.rearrange("c n o -> c (n o)"))
+        tt_sb = const.tile([P, 4, 2 * RANK], BF16, name="tt_sb")
+        nc.scalar.dma_start(
+            out=tt_sb[:], in_=tt_prefix.rearrange("(a p e) c -> p a (e c)", a=4, e=2)
+        )
+        x_of = []
+        first = 0
+        for i, count in enumerate(LOADS):
+            x_sb = xin.tile([P, count, K], BF16, name="x%d" % i)
+            nc.sync.dma_start(out=x_sb[:], in_=x_view[:, first : first + count, :])
+            for j in range(count):
+                x_of.append((x_sb, j))
+            first += count
+
+        ident_bf = const.tile([P, P], BF16, name="ident_bf")
+        make_identity(nc, ident_bf[:])
+        ident = const.tile([P, P], F32, name="ident")
+        make_identity(nc, ident[:])
+
+        w_grouped = const.tile([P, 2, N, 4], BF16, name="w_grouped", align_bytes=64)
+        w_codes = const.tile([P, 2 * N], U32, name="w_codes", align_bytes=64)
+        w_scales = const.tile([P, 2 * N], U8, name="w_scales", align_bytes=64)
+        ttT_sb = const.tile([P, 8, P], BF16, name="ttT_sb")
+
+        grouped = {}
+        codes = {}
+        scales = {}
+        acc = {}
+        xt = {}
+        out_of = {}
+        store_at = {}
+        first = 0
+        for i, count in enumerate(STORES):
+            out_sb = res.tile([P, count * QUAD, N], F32, name="out%d" % i)
+            for j in range(count):
+                out_of[first + j] = (out_sb, j)
+            store_at[first + count - 1] = (out_sb, first, count)
+            first += count
+
+        def weight_transposes():
+            ttT_ps = psum.tile([P, 8, P], BF16, name="ttT_ps", tag="acc0")
+            for j in range(8):
+                nc.tensor.transpose(
+                    ttT_ps[:, j, :],
+                    tt_sb[:, j // 2, (j % 2) * RANK : (j % 2 + 1) * RANK],
+                    ident_bf[:],
+                )
+            nc.vector.tensor_copy(out=ttT_sb[:], in_=ttT_ps[:])
+
+        def weight_product():
+            for g in range(2):
+                w_ps = psum.tile([P, 4, N], F32, name="w_ps%d" % g, tag="acc%d" % (1 - g))
+                for t in range(4):
+                    nc.tensor.matmul(
+                        w_ps[:, t, :],
+                        lhsT=ttT_sb[:, 4 * g + t, :],
+                        rhs=core_sb[:],
+                        start=True,
+                        stop=True,
+                    )
+                nc.vector.tensor_copy(
+                    out=w_grouped[:, g, :, :], in_=w_ps[:].rearrange("p t n -> p n t")
+                )
+            nc.vector.quantize_mx(
+                out=w_codes[:].bitcast(FP8X4),
+                scales=w_scales[:],
+                in_=w_grouped[:].rearrange("p g n t -> p (g n t)"),
+            )
+
+        def transposes(s):
+            grouped[s] = work.tile(
+                [P, QUAD * K], BF16, name="grouped%d" % s, tag="grouped%d" % (s % 3), align_bytes=64
+            )
+            for q in range(QUAD):
+                t = QUAD * s + q
+                x_sb, j = x_of[t]
+                words = x_sb[:, j, :].bitcast(F32)
+                xt[t] = psum.tile([P, 4, P], F32, name="xt%d" % t, tag="xt%d" % (t % XT_BANKS))
+                for b in range(4):
+                    nc.tensor.transpose(xt[t][:, b, :], words[:, b * P : (b + 1) * P], ident[:])
+
+        def copies(s):
+            dst = grouped[s][:].bitcast(F32)
+            for q in range(QUAD):
+                t = QUAD * s + q
+                d = dst[:, q * WORDS : (q + 1) * WORDS].rearrange(
+                    "p (g r u) -> p g r u", g=2, u=2
+                )
+                src = xt[t][:].rearrange("p (g u) r -> p g r u", u=2)
+                if t % 8 == 7:
+                    nc.vector.tensor_copy(out=d, in_=src)
+                else:
+                    nc.scalar.copy(out=d, in_=src)
+
+        def quantise(s):
+            codes[s] = work.tile(
+                [P, QUAD * K // 4], U32, name="codes%d" % s, tag="codes%d" % (s % 3), align_bytes=64
+            )
+            scales[s] = work.tile(
+                [P, QUAD * K // 4], U8, name="scales%d" % s, tag="scales%d" % (s % 3), align_bytes=64
+            )
+            nc.vector.quantize_mx(
+                out=codes[s][:].bitcast(FP8X4), scales=scales[s][:], in_=grouped[s][:]
+            )
+
+        def products(s):
+            acc[s] = psum.tile([P, QUAD, N], F32, name="acc%d" % s, tag="acc%d" % (s % 2))
+            for q in range(QUAD):
+                for g in range(2):
+                    c0 = (2 * q + g) * P
+                    nc.tensor.matmul_mx(
+                        out=acc[s][:, q, :],
+                        lhsT=codes[s][:, c0 : c0 + P].bitcast(FP8X4),
+                        lhsT_scale=scales[s][:, c0 : c0 + P],
+                        rhs=w_codes[:, g * N : (g + 1) * N].bitcast(FP8X4),
+                        rhs_scale=w_scales[:, g * N : (g + 1) * N],
+                        start=(g == 0),
+                        stop=(g == 1),
+                    )
+
+        def results(s):
+            out_sb, j = out_of[s]
+            nc.vector.tensor_copy(out=out_sb[:, j * QUAD : (j + 1) * QUAD, :], in_=acc[s][:])
+            if s in store_at:
+                tile_sb, first_step, count = store_at[s]
+                nc.sync.dma_start(
+                    out=out_view[:, first_step * QUAD : (first_step + count) * QUAD, :],
+                    in_=tile_sb[:],
+                )
+
+        weight_transposes()
+        for s in range(STEPS + 3):
+            if 0 <= s - 3 < STEPS:
+                results(s - 3)
+            if 0 <= s - 1 < STEPS:
+                quantise(s - 1)
+            if s < STEPS:
+                transposes(s)
+                copies(s)
+            if s == 0:
+                weight_product()
+            if 0 <= s - 2 < STEPS:
+                products(s - 2)

@@ -14,11 +14,9 @@ N = 128
 RANK = 128
 TILES = ROWS // P
 WORDS = K // 2
-QUAD = 4
-STEPS = TILES // QUAD
 XT_BANKS = 6
-LOADS = [2, 2] + [4] * 14 + [2, 2]
-STORES = [4, 4, 4, 2, 1, 1]
+UNITS = [2, 2] + [4] * 14 + [2, 2]
+STORES = [32, 16, 8, 4, 2, 2]
 
 FLOPS = 2 * ROWS * K * N + 2 * K * RANK * N
 
@@ -27,6 +25,8 @@ def tile_tttlayer_pb_t_kernel(tc, x, tt_prefix, core3, out):
     nc = tc.nc
     x_view = x.rearrange("(p t) k -> p t k", t=TILES)
     out_view = out.rearrange("(p t) n -> p t n", t=TILES)
+    start_of = [sum(UNITS[:u]) for u in range(len(UNITS))]
+    rounds = [[0], [1], [2]] + [[u, u + 1] for u in range(3, 15, 2)] + [[15], [16], [17]]
 
     with tc.tile_pool(name="const", bufs=1) as const, tc.tile_pool(
         name="xin", bufs=1
@@ -39,14 +39,12 @@ def tile_tttlayer_pb_t_kernel(tc, x, tt_prefix, core3, out):
         nc.scalar.dma_start(
             out=tt_sb[:], in_=tt_prefix.rearrange("(a p e) c -> p a (e c)", a=4, e=2)
         )
-        x_of = []
-        first = 0
-        for i, count in enumerate(LOADS):
-            x_sb = xin.tile([P, count, K], BF16, name="x%d" % i)
-            nc.sync.dma_start(out=x_sb[:], in_=x_view[:, first : first + count, :])
-            for j in range(count):
-                x_of.append((x_sb, j))
-            first += count
+        x_sb = []
+        for u, count in enumerate(UNITS):
+            x_sb.append(xin.tile([P, count, K], BF16, name="x%d" % u))
+            nc.sync.dma_start(
+                out=x_sb[u][:], in_=x_view[:, start_of[u] : start_of[u] + count, :]
+            )
 
         ident_bf = const.tile([P, P], BF16, name="ident_bf")
         make_identity(nc, ident_bf[:])
@@ -64,13 +62,13 @@ def tile_tttlayer_pb_t_kernel(tc, x, tt_prefix, core3, out):
         acc = {}
         xt = {}
         out_of = {}
-        store_at = {}
+        store_after = {}
         first = 0
         for i, count in enumerate(STORES):
-            out_sb = res.tile([P, count * QUAD, N], F32, name="out%d" % i)
+            out_sb = res.tile([P, count, N], F32, name="out%d" % i)
             for j in range(count):
                 out_of[first + j] = (out_sb, j)
-            store_at[first + count - 1] = (out_sb, first, count)
+            store_after[first + count - 1] = (out_sb, first, count)
             first += count
 
         def weight_transposes():
@@ -94,86 +92,94 @@ def tile_tttlayer_pb_t_kernel(tc, x, tt_prefix, core3, out):
                         start=True,
                         stop=True,
                     )
-                nc.vector.tensor_copy(
-                    out=w_grouped[:, g, :, :], in_=w_ps[:].rearrange("p t n -> p n t")
-                )
+                if g == 0:
+                    nc.vector.tensor_copy(
+                        out=w_grouped[:, g, :, :], in_=w_ps[:].rearrange("p t n -> p n t")
+                    )
+                else:
+                    nc.scalar.copy(
+                        out=w_grouped[:, g, :, :], in_=w_ps[:].rearrange("p t n -> p n t")
+                    )
             nc.vector.quantize_mx(
                 out=w_codes[:].bitcast(FP8X4),
                 scales=w_scales[:],
                 in_=w_grouped[:].rearrange("p g n t -> p (g n t)"),
             )
 
-        def transposes(s):
-            grouped[s] = work.tile(
-                [P, QUAD * K], BF16, name="grouped%d" % s, tag="grouped%d" % (s % 3), align_bytes=64
-            )
-            for q in range(QUAD):
-                t = QUAD * s + q
-                x_sb, j = x_of[t]
-                words = x_sb[:, j, :].bitcast(F32)
+        def transposes(u):
+            for q in range(UNITS[u]):
+                t = start_of[u] + q
+                words = x_sb[u][:, q, :].bitcast(F32)
                 xt[t] = psum.tile([P, 4, P], F32, name="xt%d" % t, tag="xt%d" % (t % XT_BANKS))
                 for b in range(4):
                     nc.tensor.transpose(xt[t][:, b, :], words[:, b * P : (b + 1) * P], ident[:])
 
-        def copies(s):
-            dst = grouped[s][:].bitcast(F32)
-            for q in range(QUAD):
-                t = QUAD * s + q
+        def copies(u, vector_takes_first):
+            grouped[u] = work.tile(
+                [P, UNITS[u] * K], BF16, name="grouped%d" % u, tag="grouped%d" % (u % 3), align_bytes=64
+            )
+            dst = grouped[u][:].bitcast(F32)
+            for q in range(UNITS[u]):
                 d = dst[:, q * WORDS : (q + 1) * WORDS].rearrange(
                     "p (g r u) -> p g r u", g=2, u=2
                 )
-                src = xt[t][:].rearrange("p (g u) r -> p g r u", u=2)
-                if t % 8 == 7:
+                src = xt[start_of[u] + q][:].rearrange("p (g u) r -> p g r u", u=2)
+                if q == 0 and vector_takes_first:
                     nc.vector.tensor_copy(out=d, in_=src)
                 else:
                     nc.scalar.copy(out=d, in_=src)
 
-        def quantise(s):
-            codes[s] = work.tile(
-                [P, QUAD * K // 4], U32, name="codes%d" % s, tag="codes%d" % (s % 3), align_bytes=64
+        def quantise(u):
+            codes[u] = work.tile(
+                [P, UNITS[u] * K // 4], U32, name="codes%d" % u, tag="codes%d" % (u % 4), align_bytes=64
             )
-            scales[s] = work.tile(
-                [P, QUAD * K // 4], U8, name="scales%d" % s, tag="scales%d" % (s % 3), align_bytes=64
+            scales[u] = work.tile(
+                [P, UNITS[u] * K // 4], U8, name="scales%d" % u, tag="scales%d" % (u % 4), align_bytes=64
             )
             nc.vector.quantize_mx(
-                out=codes[s][:].bitcast(FP8X4), scales=scales[s][:], in_=grouped[s][:]
+                out=codes[u][:].bitcast(FP8X4), scales=scales[u][:], in_=grouped[u][:]
             )
 
-        def products(s):
-            acc[s] = psum.tile([P, QUAD, N], F32, name="acc%d" % s, tag="acc%d" % (s % 2))
-            for q in range(QUAD):
+        def products(u):
+            acc[u] = psum.tile([P, UNITS[u], N], F32, name="acc%d" % u, tag="acc%d" % (u % 2))
+            for q in range(UNITS[u]):
                 for g in range(2):
                     c0 = (2 * q + g) * P
                     nc.tensor.matmul_mx(
-                        out=acc[s][:, q, :],
-                        lhsT=codes[s][:, c0 : c0 + P].bitcast(FP8X4),
-                        lhsT_scale=scales[s][:, c0 : c0 + P],
+                        out=acc[u][:, q, :],
+                        lhsT=codes[u][:, c0 : c0 + P].bitcast(FP8X4),
+                        lhsT_scale=scales[u][:, c0 : c0 + P],
                         rhs=w_codes[:, g * N : (g + 1) * N].bitcast(FP8X4),
                         rhs_scale=w_scales[:, g * N : (g + 1) * N],
                         start=(g == 0),
                         stop=(g == 1),
                     )
 
-        def results(s):
-            out_sb, j = out_of[s]
-            nc.vector.tensor_copy(out=out_sb[:, j * QUAD : (j + 1) * QUAD, :], in_=acc[s][:])
-            if s in store_at:
-                tile_sb, first_step, count = store_at[s]
+        def results(u):
+            out_sb, j = out_of[start_of[u]]
+            nc.vector.tensor_copy(out=out_sb[:, j : j + UNITS[u], :], in_=acc[u][:])
+            last = start_of[u] + UNITS[u] - 1
+            if last in store_after:
+                tile_sb, first_tile, count = store_after[last]
                 nc.sync.dma_start(
-                    out=out_view[:, first_step * QUAD : (first_step + count) * QUAD, :],
-                    in_=tile_sb[:],
+                    out=out_view[:, first_tile : first_tile + count, :], in_=tile_sb[:]
                 )
 
         weight_transposes()
-        for s in range(STEPS + 3):
-            if 0 <= s - 3 < STEPS:
-                results(s - 3)
-            if 0 <= s - 1 < STEPS:
-                quantise(s - 1)
-            if s < STEPS:
-                transposes(s)
-                copies(s)
-            if s == 0:
+        for r in range(len(rounds) + 2):
+            if 1 <= r <= len(rounds):
+                quantise(rounds[r - 1][-1])
+            if r >= 2:
+                for u in rounds[r - 2]:
+                    results(u)
+            if r < len(rounds):
+                for u in rounds[r]:
+                    transposes(u)
+                    copies(u, u == rounds[r][-1])
+                for u in rounds[r][:-1]:
+                    quantise(u)
+            if r == 0:
                 weight_product()
-            if 0 <= s - 2 < STEPS:
-                products(s - 2)
+            if 1 <= r <= len(rounds):
+                for u in rounds[r - 1]:
+                    products(u)

@@ -14,9 +14,11 @@ N = 128
 RANK = 128
 TILES = ROWS // P
 WORDS = K // 2
+QUAD = 4
+STEPS = TILES // QUAD
 XT_BANKS = 6
-UNITS = [2, 2] + [4] * 14 + [2, 2]
-STORES = [32, 16, 8, 4, 2, 2]
+LOADS = [2, 2] + [4] * 14 + [2, 2]
+STORES = [8, 4, 2, 1, 1]
 
 FLOPS = 2 * ROWS * K * N + 2 * K * RANK * N
 
@@ -25,8 +27,6 @@ def tile_tttlayer_pb_t_kernel(tc, x, tt_prefix, core3, out):
     nc = tc.nc
     x_view = x.rearrange("(p t) k -> p t k", t=TILES)
     out_view = out.rearrange("(p t) n -> p t n", t=TILES)
-    start_of = [sum(UNITS[:u]) for u in range(len(UNITS))]
-    rounds = [[0], [1], [2]] + [[u, u + 1] for u in range(3, 15, 2)] + [[15], [16], [17]]
 
     with tc.tile_pool(name="const", bufs=1) as const, tc.tile_pool(
         name="xin", bufs=1
@@ -39,12 +39,14 @@ def tile_tttlayer_pb_t_kernel(tc, x, tt_prefix, core3, out):
         nc.scalar.dma_start(
             out=tt_sb[:], in_=tt_prefix.rearrange("(a p e) c -> p a (e c)", a=4, e=2)
         )
-        x_sb = []
-        for u, count in enumerate(UNITS):
-            x_sb.append(xin.tile([P, count, K], BF16, name="x%d" % u))
-            nc.sync.dma_start(
-                out=x_sb[u][:], in_=x_view[:, start_of[u] : start_of[u] + count, :]
-            )
+        x_of = []
+        first = 0
+        for i, count in enumerate(LOADS):
+            x_sb = xin.tile([P, count, K], BF16, name="x%d" % i)
+            nc.sync.dma_start(out=x_sb[:], in_=x_view[:, first : first + count, :])
+            for j in range(count):
+                x_of.append((x_sb, j))
+            first += count
 
         ident_bf = const.tile([P, P], BF16, name="ident_bf")
         make_identity(nc, ident_bf[:])
@@ -62,13 +64,13 @@ def tile_tttlayer_pb_t_kernel(tc, x, tt_prefix, core3, out):
         acc = {}
         xt = {}
         out_of = {}
-        store_after = {}
+        store_at = {}
         first = 0
         for i, count in enumerate(STORES):
-            out_sb = res.tile([P, count, N], F32, name="out%d" % i)
+            out_sb = res.tile([P, count * QUAD, N], F32, name="out%d" % i)
             for j in range(count):
                 out_of[first + j] = (out_sb, j)
-            store_after[first + count - 1] = (out_sb, first, count)
+            store_at[first + count - 1] = (out_sb, first, count)
             first += count
 
         def weight_transposes():
@@ -92,94 +94,93 @@ def tile_tttlayer_pb_t_kernel(tc, x, tt_prefix, core3, out):
                         start=True,
                         stop=True,
                     )
-                if g == 0:
-                    nc.vector.tensor_copy(
-                        out=w_grouped[:, g, :, :], in_=w_ps[:].rearrange("p t n -> p n t")
-                    )
-                else:
-                    nc.scalar.copy(
-                        out=w_grouped[:, g, :, :], in_=w_ps[:].rearrange("p t n -> p n t")
-                    )
+                nc.vector.tensor_copy(
+                    out=w_grouped[:, g, :, :], in_=w_ps[:].rearrange("p t n -> p n t")
+                )
             nc.vector.quantize_mx(
                 out=w_codes[:].bitcast(FP8X4),
                 scales=w_scales[:],
                 in_=w_grouped[:].rearrange("p g n t -> p (g n t)"),
             )
 
-        def transposes(u):
-            for q in range(UNITS[u]):
-                t = start_of[u] + q
-                words = x_sb[u][:, q, :].bitcast(F32)
+        def transposes(s):
+            grouped[s] = work.tile(
+                [P, QUAD * K], BF16, name="grouped%d" % s, tag="grouped%d" % (s % 3), align_bytes=64
+            )
+            for q in range(QUAD):
+                t = QUAD * s + q
+                x_sb, j = x_of[t]
+                words = x_sb[:, j, :].bitcast(F32)
                 xt[t] = psum.tile([P, 4, P], F32, name="xt%d" % t, tag="xt%d" % (t % XT_BANKS))
                 for b in range(4):
                     nc.tensor.transpose(xt[t][:, b, :], words[:, b * P : (b + 1) * P], ident[:])
 
-        def copies(u, vector_takes_first):
-            grouped[u] = work.tile(
-                [P, UNITS[u] * K], BF16, name="grouped%d" % u, tag="grouped%d" % (u % 3), align_bytes=64
-            )
-            dst = grouped[u][:].bitcast(F32)
-            for q in range(UNITS[u]):
+        def copies(s):
+            dst = grouped[s][:].bitcast(F32)
+            for q in range(QUAD):
+                t = QUAD * s + q
                 d = dst[:, q * WORDS : (q + 1) * WORDS].rearrange(
                     "p (g r u) -> p g r u", g=2, u=2
                 )
-                src = xt[start_of[u] + q][:].rearrange("p (g u) r -> p g r u", u=2)
-                if q == 0 and vector_takes_first:
+                src = xt[t][:].rearrange("p (g u) r -> p g r u", u=2)
+                if q == QUAD - 1:
                     nc.vector.tensor_copy(out=d, in_=src)
                 else:
                     nc.scalar.copy(out=d, in_=src)
 
-        def quantise(u):
-            codes[u] = work.tile(
-                [P, UNITS[u] * K // 4], U32, name="codes%d" % u, tag="codes%d" % (u % 4), align_bytes=64
+        def quantise(s):
+            codes[s] = work.tile(
+                [P, QUAD * K // 4], U32, name="codes%d" % s, tag="codes%d" % (s % 3), align_bytes=64
             )
-            scales[u] = work.tile(
-                [P, UNITS[u] * K // 4], U8, name="scales%d" % u, tag="scales%d" % (u % 4), align_bytes=64
+            scales[s] = work.tile(
+                [P, QUAD * K // 4], U8, name="scales%d" % s, tag="scales%d" % (s % 3), align_bytes=64
             )
-            nc.vector.quantize_mx(
-                out=codes[u][:].bitcast(FP8X4), scales=scales[u][:], in_=grouped[u][:]
-            )
+            half = QUAD * K // 2
+            for h in range(2):
+                nc.vector.quantize_mx(
+                    out=codes[s][:, h * half // 4 : (h + 1) * half // 4].bitcast(FP8X4),
+                    scales=scales[s][:, h * half // 4 : (h + 1) * half // 4],
+                    in_=grouped[s][:, h * half : (h + 1) * half],
+                )
 
-        def products(u):
-            acc[u] = psum.tile([P, UNITS[u], N], F32, name="acc%d" % u, tag="acc%d" % (u % 2))
-            for q in range(UNITS[u]):
+        def products(s):
+            acc[s] = psum.tile([P, QUAD, N], F32, name="acc%d" % s, tag="acc%d" % (s % 2))
+            for q in range(QUAD):
                 for g in range(2):
                     c0 = (2 * q + g) * P
                     nc.tensor.matmul_mx(
-                        out=acc[u][:, q, :],
-                        lhsT=codes[u][:, c0 : c0 + P].bitcast(FP8X4),
-                        lhsT_scale=scales[u][:, c0 : c0 + P],
+                        out=acc[s][:, q, :],
+                        lhsT=codes[s][:, c0 : c0 + P].bitcast(FP8X4),
+                        lhsT_scale=scales[s][:, c0 : c0 + P],
                         rhs=w_codes[:, g * N : (g + 1) * N].bitcast(FP8X4),
                         rhs_scale=w_scales[:, g * N : (g + 1) * N],
                         start=(g == 0),
                         stop=(g == 1),
                     )
 
-        def results(u):
-            out_sb, j = out_of[start_of[u]]
-            nc.vector.tensor_copy(out=out_sb[:, j : j + UNITS[u], :], in_=acc[u][:])
-            last = start_of[u] + UNITS[u] - 1
-            if last in store_after:
-                tile_sb, first_tile, count = store_after[last]
+        def results(s):
+            out_sb, j = out_of[s]
+            if s % 2 == 1:
+                nc.scalar.copy(out=out_sb[:, j * QUAD : (j + 1) * QUAD, :], in_=acc[s][:])
+            else:
+                nc.vector.tensor_copy(out=out_sb[:, j * QUAD : (j + 1) * QUAD, :], in_=acc[s][:])
+            if s in store_at:
+                tile_sb, first_step, count = store_at[s]
                 nc.sync.dma_start(
-                    out=out_view[:, first_tile : first_tile + count, :], in_=tile_sb[:]
+                    out=out_view[:, first_step * QUAD : (first_step + count) * QUAD, :],
+                    in_=tile_sb[:],
                 )
 
         weight_transposes()
-        for r in range(len(rounds) + 2):
-            if 1 <= r <= len(rounds):
-                quantise(rounds[r - 1][-1])
-            if r >= 2:
-                for u in rounds[r - 2]:
-                    results(u)
-            if r < len(rounds):
-                for u in rounds[r]:
-                    transposes(u)
-                    copies(u, u == rounds[r][-1])
-                for u in rounds[r][:-1]:
-                    quantise(u)
-            if r == 0:
+        for s in range(STEPS + 3):
+            if 0 <= s - 3 < STEPS:
+                results(s - 3)
+            if 0 <= s - 1 < STEPS:
+                quantise(s - 1)
+            if s < STEPS:
+                transposes(s)
+                copies(s)
+            if s == 0:
                 weight_product()
-            if 1 <= r <= len(rounds):
-                for u in rounds[r - 1]:
-                    products(u)
+            if 0 <= s - 2 < STEPS:
+                products(s - 2)

@@ -34,9 +34,9 @@ def tile_tttlayer_pb_t_kernel(tc, x, tt_prefix, core3, out):
         name="res", bufs=1
     ) as res, tc.psum_pool(name="psum", bufs=1) as psum, tc.manual_schedule():
         core_sb = const.tile([P, N], BF16, name="core_sb")
-        nc.scalar.dma_start(out=core_sb[:], in_=core3.rearrange("c n o -> c (n o)"))
+        nc.sync.dma_start(out=core_sb[:], in_=core3.rearrange("c n o -> c (n o)"))
         tt_sb = const.tile([P, 4, 2 * RANK], BF16, name="tt_sb")
-        nc.scalar.dma_start(
+        nc.sync.dma_start(
             out=tt_sb[:], in_=tt_prefix.rearrange("(a p e) c -> p a (e c)", a=4, e=2)
         )
         x_of = []

import concourse.mybir as mybir
from concourse.masks import make_identity

F32 = mybir.dt.float32
BF16 = mybir.dt.bfloat16
U32 = mybir.dt.uint32
U8 = mybir.dt.uint8
FP8X4 = mybir.dt.float8_e4m3fn_x4

P = 128
ROWS = 8192
K = 1024
N = 128
RANK = 128
TILES = ROWS // P
WORDS = K // 2
QUAD = 4
STEPS = TILES // QUAD
XT_BANKS = 6
LOADS = [2, 2] + [4] * 14 + [2, 2]
STORES = [8, 4, 2, 1, 1]

FLOPS = 2 * ROWS * K * N + 2 * K * RANK * N


def tile_tttlayer_pb_t_kernel(tc, x, tt_prefix, core3, out):
    nc = tc.nc
    x_view = x.rearrange("(p t) k -> p t k", t=TILES)
    out_view = out.rearrange("(p t) n -> p t n", t=TILES)

    with tc.tile_pool(name="const", bufs=1) as const, tc.tile_pool(
        name="xin", bufs=1
    ) as xin, tc.tile_pool(name="work", bufs=1) as work, tc.tile_pool(
        name="res", bufs=1
    ) as res, tc.psum_pool(name="psum", bufs=1) as psum, tc.manual_schedule():
        core_sb = const.tile([P, N], BF16, name="core_sb")
        nc.sync.dma_start(out=core_sb[:], in_=core3.rearrange("c n o -> c (n o)"))
        tt_sb = const.tile([P, 4, 2 * RANK], BF16, name="tt_sb")
        nc.sync.dma_start(
            out=tt_sb[:], in_=tt_prefix.rearrange("(a p e) c -> p a (e c)", a=4, e=2)
        )
        x_of = []
        first = 0
        for i, count in enumerate(LOADS):
            x_sb = xin.tile([P, count, K], BF16, name="x%d" % i)
            nc.sync.dma_start(out=x_sb[:], in_=x_view[:, first : first + count, :])
            for j in range(count):
                x_of.append((x_sb, j))
            first += count

        ident_bf = const.tile([P, P], BF16, name="ident_bf")
        make_identity(nc, ident_bf[:])
        ident = const.tile([P, P], F32, name="ident")
        make_identity(nc, ident[:])

        w_grouped = const.tile([P, 2, N, 4], BF16, name="w_grouped", align_bytes=64)
        w_codes = const.tile([P, 2 * N], U32, name="w_codes", align_bytes=64)
        w_scales = const.tile([P, 2 * N], U8, name="w_scales", align_bytes=64)
        ttT_sb = const.tile([P, 8, P], BF16, name="ttT_sb")

        grouped = {}
        codes = {}
        scales = {}
        acc = {}
        xt = {}
        out_of = {}
        store_at = {}
        first = 0
        for i, count in enumerate(STORES):
            out_sb = res.tile([P, count * QUAD, N], F32, name="out%d" % i)
            for j in range(count):
                out_of[first + j] = (out_sb, j)
            store_at[first + count - 1] = (out_sb, first, count)
            first += count

        def weight_transposes():
            ttT_ps = psum.tile([P, 8, P], BF16, name="ttT_ps", tag="acc0")
            for j in range(8):
                nc.tensor.transpose(
                    ttT_ps[:, j, :],
                    tt_sb[:, j // 2, (j % 2) * RANK : (j % 2 + 1) * RANK],
                    ident_bf[:],
                )
            nc.vector.tensor_copy(out=ttT_sb[:], in_=ttT_ps[:])

        def weight_product():
            for g in range(2):
                w_ps = psum.tile([P, 4, N], F32, name="w_ps%d" % g, tag="acc%d" % (1 - g))
                for t in range(4):
                    nc.tensor.matmul(
                        w_ps[:, t, :],
                        lhsT=ttT_sb[:, 4 * g + t, :],
                        rhs=core_sb[:],
                        start=True,
                        stop=True,
                    )
                nc.vector.tensor_copy(
                    out=w_grouped[:, g, :, :], in_=w_ps[:].rearrange("p t n -> p n t")
                )
            nc.vector.quantize_mx(
                out=w_codes[:].bitcast(FP8X4),
                scales=w_scales[:],
                in_=w_grouped[:].rearrange("p g n t -> p (g n t)"),
            )

        def transposes(s):
            grouped[s] = work.tile(
                [P, QUAD * K], BF16, name="grouped%d" % s, tag="grouped%d" % (s % 3), align_bytes=64
            )
            for q in range(QUAD):
                t = QUAD * s + q
                x_sb, j = x_of[t]
                words = x_sb[:, j, :].bitcast(F32)
                xt[t] = psum.tile([P, 4, P], F32, name="xt%d" % t, tag="xt%d" % (t % XT_BANKS))
                for b in range(4):
                    nc.tensor.transpose(xt[t][:, b, :], words[:, b * P : (b + 1) * P], ident[:])

        def copies(s):
            dst = grouped[s][:].bitcast(F32)
            for q in range(QUAD):
                t = QUAD * s + q
                d = dst[:, q * WORDS : (q + 1) * WORDS].rearrange(
                    "p (g r u) -> p g r u", g=2, u=2
                )
                src = xt[t][:].rearrange("p (g u) r -> p g r u", u=2)
                if q == QUAD - 1:
                    nc.vector.tensor_copy(out=d, in_=src)
                else:
                    nc.scalar.copy(out=d, in_=src)

        def quantise(s):
            codes[s] = work.tile(
                [P, QUAD * K // 4], U32, name="codes%d" % s, tag="codes%d" % (s % 3), align_bytes=64
            )
            scales[s] = work.tile(
                [P, QUAD * K // 4], U8, name="scales%d" % s, tag="scales%d" % (s % 3), align_bytes=64
            )
            half = QUAD * K // 2
            for h in range(2):
                nc.vector.quantize_mx(
                    out=codes[s][:, h * half // 4 : (h + 1) * half // 4].bitcast(FP8X4),
                    scales=scales[s][:, h * half // 4 : (h + 1) * half // 4],
                    in_=grouped[s][:, h * half : (h + 1) * half],
                )

        def products(s):
            acc[s] = psum.tile([P, QUAD, N], F32, name="acc%d" % s, tag="acc%d" % (s % 2))
            for q in range(QUAD):
                for g in range(2):
                    c0 = (2 * q + g) * P
                    nc.tensor.matmul_mx(
                        out=acc[s][:, q, :],
                        lhsT=codes[s][:, c0 : c0 + P].bitcast(FP8X4),
                        lhsT_scale=scales[s][:, c0 : c0 + P],
                        rhs=w_codes[:, g * N : (g + 1) * N].bitcast(FP8X4),
                        rhs_scale=w_scales[:, g * N : (g + 1) * N],
                        start=(g == 0),
                        stop=(g == 1),
                    )

        def results(s):
            out_sb, j = out_of[s]
            if s % 2 == 1:
                nc.scalar.copy(out=out_sb[:, j * QUAD : (j + 1) * QUAD, :], in_=acc[s][:])
            else:
                nc.vector.tensor_copy(out=out_sb[:, j * QUAD : (j + 1) * QUAD, :], in_=acc[s][:])
            if s in store_at:
                tile_sb, first_step, count = store_at[s]
                nc.sync.dma_start(
                    out=out_view[:, first_step * QUAD : (first_step + count) * QUAD, :],
                    in_=tile_sb[:],
                )

        weight_transposes()
        for s in range(STEPS + 3):
            if 0 <= s - 3 < STEPS:
                results(s - 3)
            if 0 <= s - 1 < STEPS:
                quantise(s - 1)
            if s < STEPS:
                transposes(s)
                copies(s)
            if s == 0:
                weight_product()
            if 0 <= s - 2 < STEPS:
                products(s - 2)
